import numpy as np
import ml_dtypes


def mxq(x, axis, fmt="e4m3"):
    dtype, down = {"e4m3": (ml_dtypes.float8_e4m3fn, 7), "e5m2": (ml_dtypes.float8_e5m2, 14)}[fmt]
    v = np.moveaxis(np.asarray(x, np.float32).astype(ml_dtypes.bfloat16).astype(np.float64), axis, -1)
    blocks = v.reshape(v.shape[:-1] + (-1, 32))
    amax = np.abs(blocks).max(-1, keepdims=True)
    byte = np.maximum(np.where(amax > 0, np.frexp(amax)[1] - 1 + 127, 0) - down, 1)
    scale = np.exp2(byte - 127.0)
    codes = (blocks / scale).astype(np.float32).astype(dtype).astype(np.float64)
    return np.moveaxis((codes * scale).reshape(v.shape), -1, axis)


WIDE = False


def mx_kscale(k):
    if not WIDE:
        return np.ones(k)
    levels = np.array([10, -10, 5, -5, 0])
    if k % 512:
        return np.exp2(np.random.permutation(np.resize(levels, k // 32))).repeat(32)
    a = np.empty((k // 512, 16))
    for p in range(k // 512):
        a[p, :8] = np.random.permutation(np.resize(levels, 8))
        for g in range(8):
            far = levels[np.abs(levels - a[p, g]) >= 10]
            a[p, g + 8] = far[np.random.randint(len(far))]
    return np.exp2(a.ravel()).repeat(32)


BF16 = ml_dtypes.bfloat16


def bf(x):
    return np.asarray(x, np.float32).astype(BF16)


def f64(x):
    return np.asarray(x).astype(np.float64)


DIM, H, HD, KV, B, S = 1024, 8, 128, 2, 4, 512
T = B * S
THETA = 10000.0


def apply_rope(t, cos, sin):
    tr = t.reshape(t.shape[0], t.shape[1], -1, 2)
    t1, t2 = tr[..., 0], tr[..., 1]
    c = cos[:, None, :]
    s = sin[:, None, :]
    o1 = t1 * c - t2 * s
    o2 = t1 * s + t2 * c
    return np.stack([o1, o2], axis=-1).reshape(t.shape)


def draw0():
    s = mx_kscale(DIM)
    inv_freq = 1.0 / THETA ** (np.arange(0, HD, 2) / HD)
    pos = np.tile(np.arange(S), B)
    angles = pos[:, None] * inv_freq[None, :]
    return {"x": bf(np.random.standard_normal((T, DIM)) * s),
            "freqs_cos": bf(np.cos(angles)),
            "freqs_sin": bf(np.sin(angles)),
            "wq": bf(np.random.standard_normal((DIM, H * HD)) * 1.4 / np.sqrt(DIM) / s[:, None]),
            "wk": bf(np.random.standard_normal((DIM, KV * HD)) * 1.4 / np.sqrt(DIM) / s[:, None]),
            "wv": bf(np.random.standard_normal((DIM, KV * HD)) / np.sqrt(DIM) / s[:, None])}


def core(x, freqs_cos, freqs_sin, wq, wk, wv):
    xm = mxq(f64(x), 1, "e4m3")
    q = (xm @ mxq(f64(wq), 0, "e4m3")).reshape(T, H, HD)
    k = (xm @ mxq(f64(wk), 0, "e4m3")).reshape(T, KV, HD)
    v = (xm @ mxq(f64(wv), 0, "e4m3")).reshape(T, KV, HD)
    c, s = f64(freqs_cos), f64(freqs_sin)
    return apply_rope(q, c, s), apply_rope(k, c, s), v


def e4m3fn_bytes(y):
    return np.clip(np.asarray(y, np.float64), -448.0, 448.0).astype(np.float32).astype(ml_dtypes.float8_e4m3fn).view(np.uint8)


def e4m3fn_values(b):
    return np.asarray(b, np.uint8).view(ml_dtypes.float8_e4m3fn).astype(np.float64)


def setup_inputs():
    d = draw0()
    x0 = np.asarray(d['x']).astype(np.float64)
    s = (np.max(np.abs(x0), axis=(0,), keepdims=True) / 448.0).astype(np.float32)
    out = {}
    for k, v in d.items():
        if k == 'x':
            out['x_bytes'] = e4m3fn_bytes(x0 / s.astype(np.float64))
            out['x_scale'] = s
        else:
            out[k] = v
    return out


def reference(x_bytes, x_scale, freqs_cos, freqs_sin, wq, wk, wv):
    return core(e4m3fn_values(x_bytes) * x_scale.astype(np.float64), freqs_cos, freqs_sin, wq, wk, wv)

@@ -1,0 +1,333 @@
+from contextlib import ExitStack
+
+import concourse.mybir as mybir
+from concourse.masks import make_identity
+
+F32 = mybir.dt.float32
+BF16 = mybir.dt.bfloat16
+U32 = mybir.dt.uint32
+U8 = mybir.dt.uint8
+FP8 = mybir.dt.float8_e4m3fn
+FP8X4 = mybir.dt.float8_e4m3fn_x4
+MULT = mybir.AluOpType.mult
+ADD = mybir.AluOpType.add
+
+T, DIM, HD = 2048, 1024, 128
+FLOPS = 2 * T * DIM * 1536
+
+P = 128
+NT = T // P
+NPAIR = NT // 2
+UNITS = (("q", 0, 0), ("q", 1, 0), ("k", 0, 0), ("q", 0, 1), ("q", 1, 1), ("v", 0, 0))
+XS = (2, 3, 4, 5, 6, 7)
+COPY = mybir.ActivationFunctionType.Copy
+
+
+def tile_attention_pa_kernel(
+    tc, x_bytes, x_scale, freqs_cos, freqs_sin, wq, wk, wv, out_0, out_1, out_2
+):
+    nc = tc.nc
+    with ExitStack() as ctx:
+        ctx.enter_context(tc.manual_schedule())
+        const = ctx.enter_context(tc.tile_pool(name="const", bufs=1))
+        wpool = ctx.enter_context(tc.tile_pool(name="wpool", bufs=1))
+        xbp = ctx.enter_context(tc.tile_pool(name="xbp", bufs=1))
+        xwork = ctx.enter_context(tc.tile_pool(name="xwork", bufs=3))
+        rope = ctx.enter_context(tc.tile_pool(name="rope", bufs=4))
+        outp = ctx.enter_context(tc.tile_pool(name="outp", bufs=5))
+        accp = ctx.enter_context(tc.psum_pool(name="accp", bufs=6))
+        xtp = ctx.enter_context(tc.psum_pool(name="xtp", bufs=1))
+
+        xb_v = x_bytes.rearrange("(p i) k -> p i k", i=NT)
+        q_v = out_0.rearrange("(p i) h d -> p i (h d)", i=NT)
+        k_v = out_1.rearrange("(p i) h d -> p i (h d)", i=NT)
+        v_v = out_2.rearrange("(p i) h d -> p i (h d)", i=NT)
+        wq_v = wq.rearrange("(g p t) n -> g p t n", p=P, t=4)
+
+        xb = []
+        for n in range(NPAIR):
+            xb.append(xbp.tile([P, 2, DIM], U8, name="xbytes%d" % n, tag="xbytes%d" % n))
+        sc = const.tile([P, 2, 4], F32, name="sc", tag="sc")
+        cosr = const.tile([P, NT, 64], BF16, name="cosr", tag="cosr")
+        ss = const.tile([P, 2, NT, 64], BF16, name="ss", tag="ss")
+        wraw = {}
+        for key in ("q00", "q01", "q10", "q11", "k", "v"):
+            wraw[key] = wpool.tile([P, 2048], BF16, name="wraw" + key, tag="wraw" + key)
+
+        def load_x(n):
+            nc.sync.dma_start(out=xb[n][:], in_=xb_v[:, 2 * n : 2 * n + 2, :])
+
+        def load_wq(c, g):
+            nc.sync.dma_start(
+                out=wraw["q%d%d" % (c, g)][:].rearrange("p (t n) -> p t n", t=4),
+                in_=wq_v[g][:, :, c * 512 : (c + 1) * 512],
+            )
+
+        def load_wkv(key, w):
+            nc.sync.dma_start(
+                out=wraw[key][:].rearrange("p (g t n) -> p g t n", g=2, t=4),
+                in_=w.rearrange("(g p t) n -> p g t n", p=P, t=4),
+            )
+
+        load_x(0)
+        nc.sync.dma_start(out=sc[:], in_=x_scale.rearrange("o (g p t) -> p (o g) t", p=P, t=4))
+        load_wq(0, 0)
+        load_wq(0, 1)
+        load_x(1)
+        nc.sync.dma_start(out=cosr[:], in_=freqs_cos.rearrange("(p i) j -> p i j", i=NT))
+        nc.sync.dma_start(out=ss[:, 1, :, :], in_=freqs_sin.rearrange("(p i) j -> p i j", i=NT))
+        load_wkv("k", wk)
+        load_wq(1, 0)
+        load_wq(1, 1)
+        load_wkv("v", wv)
+        for n in range(2, NPAIR):
+            load_x(n)
+
+        ident = const.tile([P, P], F32, name="ident", tag="ident")
+        make_identity(nc, ident[:])
+        warm = const.tile([P, 1], F32, name="warm", tag="warm")
+        nc.scalar.activation(out=warm[:], in_=ident[:, 0:1], func=COPY)
+
+        wc = {}
+        ws = {}
+        wg = {}
+
+        def interleave_w(key, eng):
+            grouped = wpool.tile([P, 2048], BF16, name="wg" + key, tag="wg" + key, align_bytes=64)
+            wg[key] = grouped
+            if key in ("k", "v"):
+                o = grouped[:].rearrange("p (g n t) -> p g n t", g=2, t=4)
+                i = wraw[key][:].rearrange("p (g t n) -> p g n t", g=2, t=4)
+            else:
+                o = grouped[:].rearrange("p (n t) -> p n t", t=4)
+                i = wraw[key][:].rearrange("p (t n) -> p n t", t=4)
+            if eng == "v":
+                nc.vector.tensor_copy(out=o, in_=i)
+            elif eng == "g":
+                nc.gpsimd.tensor_scalar(out=o, in0=i, scalar1=1.0, scalar2=0.0, op0=MULT, op1=ADD)
+            else:
+                nc.scalar.copy(out=o, in_=i)
+
+        def quantize_w(key):
+            codes = wpool.tile([P, 512], U32, name="wc" + key, tag="wc" + key, align_bytes=64)
+            scales = wpool.tile([P, 512], U8, name="ws" + key, tag="ws" + key, align_bytes=64)
+            wc[key] = codes
+            ws[key] = scales
+            nc.vector.quantize_mx(out=codes[:].bitcast(FP8X4), scales=scales[:], in_=wg[key][:])
+
+        xbf = {}
+        xt = {}
+        xg = {}
+        xc = {}
+        xs = {}
+        acc = {}
+
+        def cast(n):
+            t = xwork.tile([P, 2 * DIM], BF16, name="xbf", tag="xbf")
+            xbf[n] = t
+            nc.scalar.copy(out=t[:], in_=xb[n][:].rearrange("p i k -> p (i k)").bitcast(FP8))
+
+        def transposes(n, g):
+            words = xbf[n][:].bitcast(F32)
+            t = xtp.tile([P, 2, 256], F32, name="xt%d" % g, tag="xt%d" % g)
+            xt[(n, g)] = t
+            for u in range(2):
+                for tl in range(2):
+                    lo = tl * 512 + 256 * g + u
+                    nc.tensor.transpose(
+                        t[:, u, tl * P : (tl + 1) * P],
+                        words[:, lo : tl * 512 + 256 * (g + 1) : 2],
+                        ident[:],
+                    )
+
+        def scale_out_s(n, g):
+            if n not in xg:
+                xg[n] = xwork.tile([P, 2048], BF16, name="xg", tag="xg", align_bytes=64)
+            src = xt[(n, g)][:].rearrange("p u r -> p (u r)").bitcast(BF16).rearrange("p (u r e) -> p u r e", u=2, e=2)
+            dst = xg[n][:, g * 1024 : (g + 1) * 1024].rearrange("p (r t) -> p r t", t=4)
+            for t in range(4):
+                nc.scalar.activation(
+                    out=dst[:, :, t], in_=src[:, t // 2, :, t % 2], func=COPY, scale=sc[:, g, t : t + 1]
+                )
+
+        def scale_out(n, g):
+            if n not in xg:
+                xg[n] = xwork.tile([P, 2048], BF16, name="xg", tag="xg", align_bytes=64)
+            src = xt[(n, g)][:].rearrange("p u r -> p (u r)").bitcast(BF16)
+            nc.vector.tensor_tensor(
+                out=xg[n][:, g * 1024 : (g + 1) * 1024].rearrange("p (r u e) -> p r u e", u=2, e=2),
+                in0=src.rearrange("p (u r e) -> p r u e", u=2, e=2),
+                in1=sc[:, g, :].rearrange("p (u e) -> p u e", e=2).unsqueeze(1).to_broadcast([P, 256, 2, 2]),
+                op=MULT,
+            )
+
+        def quantize_x(n, g):
+            if n not in xc:
+                xc[n] = xwork.tile([P, 512], U32, name="xc", tag="xc", align_bytes=64)
+                xs[n] = xwork.tile([P, 512], U8, name="xs", tag="xs", align_bytes=64)
+            nc.vector.quantize_mx(
+                out=xc[n][:, g * 256 : (g + 1) * 256].bitcast(FP8X4),
+                scales=xs[n][:, g * 256 : (g + 1) * 256],
+                in_=xg[n][:, g * 1024 : (g + 1) * 1024],
+            )
+
+        def mm(n, u):
+            kind, tl, c = UNITS[u]
+            a = accp.tile([P, 512], F32, name="acc", tag="acc")
+            acc[(n, u)] = a
+            if kind == "q":
+                for g in range(2):
+                    cols = slice(g * 256 + tl * P, g * 256 + (tl + 1) * P)
+                    key = "q%d%d" % (c, g)
+                    nc.tensor.matmul_mx(
+                        out=a[:],
+                        lhsT=xc[n][:, cols].bitcast(FP8X4),
+                        lhsT_scale=xs[n][:, cols],
+                        rhs=wc[key][:].bitcast(FP8X4),
+                        rhs_scale=ws[key][:],
+                        start=(g == 0),
+                        stop=(g == 1),
+                    )
+            else:
+                for t2 in range(2):
+                    for g in range(2):
+                        cols = slice(g * 256 + t2 * P, g * 256 + (t2 + 1) * P)
+                        wcols = slice(g * 256, (g + 1) * 256)
+                        nc.tensor.matmul_mx(
+                            out=a[:, t2 * 256 : (t2 + 1) * 256],
+                            lhsT=xc[n][:, cols].bitcast(FP8X4),
+                            lhsT_scale=xs[n][:, cols],
+                            rhs=wc[kind][:, wcols].bitcast(FP8X4),
+                            rhs_scale=ws[kind][:, wcols],
+                            start=(g == 0),
+                            stop=(g == 1),
+                        )
+
+        def rot_part(a_ap, b_ap, u_ap, i, nh):
+            pat = "p (h j e) -> p h j e"
+            shape = [P, nh, 64, 2]
+            nc.vector.tensor_tensor(
+                out=a_ap.rearrange(pat, j=64, e=2),
+                in0=u_ap.rearrange(pat, j=64, e=2),
+                in1=cosr[:, i, :].unsqueeze(1).unsqueeze(3).to_broadcast(shape),
+                op=MULT,
+            )
+            nc.vector.tensor_tensor(
+                out=b_ap.rearrange(pat, j=64, e=2),
+                in0=u_ap.rearrange(pat, j=64, e=2)[:, :, :, ::-1],
+                in1=ss[:, :, i, :].rearrange("p e j -> p j e").unsqueeze(1).to_broadcast(shape),
+                op=MULT,
+            )
+
+        kt = {}
+
+        def add_store(n, u, ta, tb, on_vector):
+            kind, tl, c = UNITS[u]
+            o = outp.tile([P, 512], F32, name="o", tag="o")
+            if on_vector:
+                nc.vector.tensor_tensor(out=o[:], in0=ta[:], in1=tb[:], op=ADD)
+            else:
+                nc.gpsimd.tensor_tensor(out=o[:], in0=ta[:], in1=tb[:], op=ADD)
+            if kind == "q":
+                nc.sync.dma_start(out=q_v[:, 2 * n + tl, c * 512 : (c + 1) * 512], in_=o[:])
+            else:
+                nc.sync.dma_start(out=k_v[:, 2 * n : 2 * n + 2, :], in_=o[:].rearrange("p (a f) -> p a f", a=2))
+
+        def rot_k(n, u):
+            a = acc[(n, u)]
+            ta = rope.tile([P, 512], F32, name="ta", tag="ta")
+            tb = rope.tile([P, 512], F32, name="tb", tag="tb")
+            kt[n] = (ta, tb)
+            for half in range(2):
+                cs = slice(half * 256, (half + 1) * 256)
+                rot_part(ta[:, cs], tb[:, cs], a[:, cs], 2 * n + half, 2)
+
+        def add_k(n, u):
+            add_store(n, u, kt[n][0], kt[n][1], False)
+
+        def finish(n, u, on_vector=False):
+            kind, tl, c = UNITS[u]
+            a = acc[(n, u)]
+            if kind == "v":
+                o = outp.tile([P, 512], F32, name="ov", tag="ov")
+                nc.scalar.copy(out=o[:], in_=a[:])
+                nc.scalar.dma_start(out=v_v[:, 2 * n : 2 * n + 2, :], in_=o[:].rearrange("p (a f) -> p a f", a=2))
+                return
+            ta = rope.tile([P, 512], F32, name="ta", tag="ta")
+            tb = rope.tile([P, 512], F32, name="tb", tag="tb")
+            rot_part(ta[:], tb[:], a[:], 2 * n + tl, 4)
+            add_store(n, u, ta, tb, on_vector)
+
+        cast(0)
+        transposes(0, 0)
+        transposes(0, 1)
+        interleave_w("q00", "v")
+        interleave_w("q01", "v")
+        scale_out(0, 0)
+        scale_out(0, 1)
+        quantize_w("q00")
+        quantize_w("q01")
+        quantize_x(0, 0)
+        quantize_x(0, 1)
+        cast(1)
+        nc.vector.tensor_scalar(out=ss[:, 0, :, :], in0=ss[:, 1, :, :], scalar1=-1.0, scalar2=0.0, op0=MULT, op1=ADD)
+        interleave_w("k", "s")
+        interleave_w("q10", "s")
+        interleave_w("q11", "s")
+        cast(2)
+        cast(3)
+        transposes(1, 0)
+        transposes(1, 1)
+        mm(0, 0)
+        mm(0, 1)
+        scale_out(1, 0)
+
+        for n in range(NPAIR):
+            more = n + 1 < NPAIR
+            early = (n + 2 in XS) and (n + 1 in XS)
+            if early:
+                transposes(n + 2, 1)
+                scale_out_s(n + 2, 1)
+            finish(n, 0)
+            finish(n, 1)
+            if n == 0:
+                scale_out(1, 1)
+                quantize_w("k")
+                mm(0, 2)
+                quantize_w("q10")
+                quantize_w("q11")
+                mm(0, 3)
+                mm(0, 4)
+                interleave_w("v", "v")
+                quantize_x(1, 1)
+                quantize_x(1, 0)
+                quantize_w("v")
+                mm(0, 5)
+                transposes(2, 1)
+                scale_out_s(2, 1)
+                rot_k(0, 2)
+                add_k(0, 2)
+            else:
+                if more:
+                    scale_out(n + 1, 0)
+                rot_k(n, 2)
+                if more:
+                    quantize_x(n + 1, 1)
+                    quantize_x(n + 1, 0)
+                add_k(n, 2)
+            if more:
+                mm(n + 1, 0)
+                mm(n + 1, 1)
+                mm(n + 1, 2)
+            if n + 2 < NPAIR:
+                transposes(n + 2, 0)
+            finish(n, 5)
+            if n + 4 < NPAIR:
+                cast(n + 4)
+            finish(n, 3)
+            if more:
+                mm(n + 1, 3)
+            finish(n, 4, not more)
+            if more:
+                mm(n + 1, 4)
+                mm(n + 1, 5)

@@ -270,10 +270,11 @@ def tile_attention_pa_kernel(
         quantize_x(0, 0)
         quantize_x(0, 1)
         cast(1)
-        nc.vector.tensor_scalar(out=ss[:, 0, :, :], in0=ss[:, 1, :, :], scalar1=-1.0, scalar2=0.0, op0=MULT, op1=ADD)
         interleave_w("k", "s")
+        nc.scalar.activation(out=ss[:, 0, :, :], in_=ss[:, 1, :, :], func=COPY, scale=-1.0)
         interleave_w("q10", "s")
         interleave_w("q11", "s")
+        interleave_w("v", "s")
         cast(2)
         cast(3)
         transposes(1, 0)
@@ -298,7 +299,6 @@ def tile_attention_pa_kernel(
                 quantize_w("q11")
                 mm(0, 3)
                 mm(0, 4)
-                interleave_w("v", "v")
                 quantize_x(1, 1)
                 quantize_x(1, 0)
                 quantize_w("v")

@@ -99,8 +99,8 @@ def tile_attention_pa_kernel(
                 o = grouped[:].rearrange("p (g n t) -> p g n t", g=2, t=4)
                 i = wraw[key][:].rearrange("p (g t n) -> p g n t", g=2, t=4)
             else:
-                o = grouped[:].rearrange("p (n t) -> p n t", t=4)
-                i = wraw[key][:].rearrange("p (t n) -> p n t", t=4)
+                o = grouped[:].rearrange("p (c i t) -> p c t i", i=4, t=4)
+                i = wraw[key][:].rearrange("p (t c i) -> p c t i", t=4, i=4)
             if eng == "v":
                 nc.vector.tensor_copy(out=o, in_=i)
             elif eng == "g":

@@ -122,10 +122,13 @@ def tile_attention_pa_kernel(
         xs = {}
         acc = {}
 
-        def cast(n):
+        def cast(n, on_vector=False):
             t = xwork.tile([P, 2 * DIM], BF16, name="xbf", tag="xbf")
             xbf[n] = t
-            nc.scalar.copy(out=t[:], in_=xb[n][:].rearrange("p i k -> p (i k)").bitcast(FP8))
+            if on_vector:
+                nc.vector.tensor_copy(out=t[:], in_=xb[n][:].rearrange("p i k -> p (i k)").bitcast(FP8))
+            else:
+                nc.scalar.copy(out=t[:], in_=xb[n][:].rearrange("p i k -> p (i k)").bitcast(FP8))
 
         def transposes(n, g):
             words = xbf[n][:].bitcast(F32)
@@ -258,7 +261,7 @@ def tile_attention_pa_kernel(
             rot_part(ta[:], tb[:], a[:], 2 * n + tl, 4)
             add_store(n, u, ta, tb, on_vector)
 
-        cast(0)
+        cast(0, True)
         transposes(0, 0)
         transposes(0, 1)
         interleave_w("q00", "v")

@@ -273,8 +273,8 @@ def tile_attention_pa_kernel(
         quantize_x(0, 0)
         quantize_x(0, 1)
         cast(1)
+        nc.vector.tensor_scalar(out=ss[:, 0, :, :], in0=ss[:, 1, :, :], scalar1=-1.0, scalar2=0.0, op0=MULT, op1=ADD)
         interleave_w("k", "s")
-        nc.scalar.activation(out=ss[:, 0, :, :], in_=ss[:, 1, :, :], func=COPY, scale=-1.0)
         interleave_w("q10", "s")
         interleave_w("q11", "s")
         interleave_w("v", "s")

@@ -191,7 +191,7 @@ def tile_attention_pa_kernel(
                         start=(g == 0),
                         stop=(g == 1),
                     )
-            else:
+            elif kind == "v":
                 for t2 in range(2):
                     for g in range(2):
                         cols = slice(g * 256 + t2 * P, g * 256 + (t2 + 1) * P)
@@ -205,6 +205,21 @@ def tile_attention_pa_kernel(
                             start=(g == 0),
                             stop=(g == 1),
                         )
+            else:
+                for t2 in range(2):
+                    for h in range(2):
+                        for g in range(2):
+                            cols = slice(g * 256 + t2 * P, g * 256 + (t2 + 1) * P)
+                            wcols = slice(g * 256 + h * P, g * 256 + (h + 1) * P)
+                            nc.tensor.matmul_mx(
+                                out=a[:, h * 256 + t2 * P : h * 256 + (t2 + 1) * P],
+                                lhsT=xc[n][:, cols].bitcast(FP8X4),
+                                lhsT_scale=xs[n][:, cols],
+                                rhs=wc[kind][:, wcols].bitcast(FP8X4),
+                                rhs_scale=ws[kind][:, wcols],
+                                start=(g == 0),
+                                stop=(g == 1),
+                            )
 
         def rot_part(a_ap, b_ap, u_ap, i, nh):
             pat = "p (h j e) -> p h j e"
@@ -234,16 +249,31 @@ def tile_attention_pa_kernel(
             if kind == "q":
                 nc.sync.dma_start(out=q_v[:, 2 * n + tl, c * 512 : (c + 1) * 512], in_=o[:])
             else:
-                nc.sync.dma_start(out=k_v[:, 2 * n : 2 * n + 2, :], in_=o[:].rearrange("p (a f) -> p a f", a=2))
+                for h in range(2):
+                    nc.sync.dma_start(
+                        out=k_v[:, 2 * n : 2 * n + 2, h * P : (h + 1) * P],
+                        in_=o[:, h * 256 : (h + 1) * 256].rearrange("p (a f) -> p a f", a=2),
+                    )
 
         def rot_k(n, u):
             a = acc[(n, u)]
             ta = rope.tile([P, 512], F32, name="ta", tag="ta")
             tb = rope.tile([P, 512], F32, name="tb", tag="tb")
             kt[n] = (ta, tb)
-            for half in range(2):
-                cs = slice(half * 256, (half + 1) * 256)
-                rot_part(ta[:, cs], tb[:, cs], a[:, cs], 2 * n + half, 2)
+            pat = "p (h j e) -> p h j e"
+            shape = [P, 2, 128, 2]
+            nc.vector.tensor_tensor(
+                out=ta[:].rearrange(pat, j=128, e=2),
+                in0=a[:].rearrange(pat, j=128, e=2),
+                in1=cosr[:, 2 * n : 2 * n + 2, :].rearrange("p i j -> p (i j)").unsqueeze(1).unsqueeze(3).to_broadcast(shape),
+                op=MULT,
+            )
+            nc.vector.tensor_tensor(
+                out=tb[:].rearrange(pat, j=128, e=2),
+                in0=a[:].rearrange(pat, j=128, e=2)[:, :, :, ::-1],
+                in1=ss[:, :, 2 * n : 2 * n + 2, :].rearrange("p e i j -> p (i j) e").unsqueeze(1).to_broadcast(shape),
+                op=MULT,
+            )
 
         def add_k(n, u):
             add_store(n, u, kt[n][0], kt[n][1], False)

@@ -85,6 +85,8 @@ def tile_attention_pa_kernel(
 
         ident = const.tile([P, P], F32, name="ident", tag="ident")
         make_identity(nc, ident[:])
+        identb = const.tile([P, P], BF16, name="identb", tag="identb")
+        make_identity(nc, identb[:])
         warm = const.tile([P, 1], F32, name="warm", tag="warm")
         nc.scalar.activation(out=warm[:], in_=ident[:, 0:1], func=COPY)
 
@@ -120,6 +122,8 @@ def tile_attention_pa_kernel(
         xg = {}
         xc = {}
         xs = {}
+        pl = {}
+        il = {}
         acc = {}
 
         def cast(n, on_vector=False):
@@ -143,15 +147,31 @@ def tile_attention_pa_kernel(
                         ident[:],
                     )
 
-        def scale_out_s(n, g):
-            if n not in xg:
-                xg[n] = xwork.tile([P, 2048], BF16, name="xg", tag="xg", align_bytes=64)
+        def planes(n, g):
+            t4 = xwork.tile([P, 4, 256], BF16, name="pl%d" % g, tag="pl%d" % g)
+            pl[(n, g)] = t4
             src = xt[(n, g)][:].rearrange("p u r -> p (u r)").bitcast(BF16).rearrange("p (u r e) -> p u r e", u=2, e=2)
-            dst = xg[n][:, g * 1024 : (g + 1) * 1024].rearrange("p (r t) -> p r t", t=4)
             for t in range(4):
                 nc.scalar.activation(
-                    out=dst[:, :, t], in_=src[:, t // 2, :, t % 2], func=COPY, scale=sc[:, g, t : t + 1]
+                    out=t4[:, t, :], in_=src[:, t // 2, :, t % 2], func=COPY, scale=sc[:, g, t : t + 1]
                 )
+
+        def weave(n, g):
+            bank = xtp.tile([P, 1024], BF16, name="xt%d" % g, tag="xt%d" % g)
+            il[(n, g)] = bank
+            for h in range(2):
+                nc.tensor.matmul(
+                    bank[:, h * 512 : (h + 1) * 512],
+                    lhsT=identb[:],
+                    rhs=pl[(n, g)][:, :, h * P : (h + 1) * P].rearrange("p t r -> p r t"),
+                    start=True,
+                    stop=True,
+                )
+
+        def weave_out(n, g):
+            if n not in xg:
+                xg[n] = xwork.tile([P, 2048], BF16, name="xg", tag="xg", align_bytes=64)
+            nc.scalar.copy(out=xg[n][:, g * 1024 : (g + 1) * 1024], in_=il[(n, g)][:])
 
         def scale_out(n, g):
             if n not in xg:
@@ -321,7 +341,7 @@ def tile_attention_pa_kernel(
             early = (n + 2 in XS) and (n + 1 in XS)
             if early:
                 transposes(n + 2, 1)
-                scale_out_s(n + 2, 1)
+                planes(n + 2, 1)
             finish(n, 0)
             finish(n, 1)
             if n == 0:
@@ -337,7 +357,7 @@ def tile_attention_pa_kernel(
                 quantize_w("v")
                 mm(0, 5)
                 transposes(2, 1)
-                scale_out_s(2, 1)
+                planes(2, 1)
                 rot_k(0, 2)
                 add_k(0, 2)
             else:
@@ -354,7 +374,10 @@ def tile_attention_pa_kernel(
                 mm(n + 1, 2)
             if n + 2 < NPAIR:
                 transposes(n + 2, 0)
+                weave(n + 2, 1)
             finish(n, 5)
+            if n + 2 < NPAIR:
+                weave_out(n + 2, 1)
             if n + 4 < NPAIR:
                 cast(n + 4)
             finish(n, 3)

@@ -20,6 +20,7 @@ NT = T // P
 NPAIR = NT // 2
 UNITS = (("q", 0, 0), ("q", 1, 0), ("k", 0, 0), ("q", 0, 1), ("q", 1, 1), ("v", 0, 0))
 XS = (2, 3, 4, 5, 6, 7)
+WOVEN0 = (7,)
 COPY = mybir.ActivationFunctionType.Copy
 
 
@@ -295,10 +296,10 @@ def tile_attention_pa_kernel(
                 op=MULT,
             )
 
-        def add_k(n, u):
-            add_store(n, u, kt[n][0], kt[n][1], False)
+        def add_k(n, u, on_vector=False):
+            add_store(n, u, kt[n][0], kt[n][1], on_vector)
 
-        def finish(n, u, on_vector=False):
+        def finish(n, u, later=False):
             kind, tl, c = UNITS[u]
             a = acc[(n, u)]
             if kind == "v":
@@ -309,19 +310,21 @@ def tile_attention_pa_kernel(
             ta = rope.tile([P, 512], F32, name="ta", tag="ta")
             tb = rope.tile([P, 512], F32, name="tb", tag="tb")
             rot_part(ta[:], tb[:], a[:], 2 * n + tl, 4)
-            add_store(n, u, ta, tb, on_vector)
+            if not later:
+                add_store(n, u, ta, tb, False)
+            return ta, tb
 
         cast(0, True)
         transposes(0, 0)
         transposes(0, 1)
-        interleave_w("q00", "v")
+        interleave_w("q00", "s")
         interleave_w("q01", "v")
         scale_out(0, 0)
         scale_out(0, 1)
-        quantize_w("q00")
-        quantize_w("q01")
         quantize_x(0, 0)
+        quantize_w("q00")
         quantize_x(0, 1)
+        quantize_w("q01")
         cast(1)
         nc.vector.tensor_scalar(out=ss[:, 0, :, :], in0=ss[:, 1, :, :], scalar1=-1.0, scalar2=0.0, op0=MULT, op1=ADD)
         interleave_w("k", "s")
@@ -330,60 +333,75 @@ def tile_attention_pa_kernel(
         interleave_w("v", "s")
         cast(2)
         cast(3)
-        transposes(1, 0)
-        transposes(1, 1)
         mm(0, 0)
         mm(0, 1)
-        scale_out(1, 0)
+        transposes(1, 0)
+        transposes(1, 1)
 
-        for n in range(NPAIR):
-            more = n + 1 < NPAIR
+        for n in range(NPAIR - 1):
             early = (n + 2 in XS) and (n + 1 in XS)
             if early:
                 transposes(n + 2, 1)
                 planes(n + 2, 1)
             finish(n, 0)
-            finish(n, 1)
+            wide = n + 1 in WOVEN0
+            late_add = finish(n, 1, wide)
             if n == 0:
+                scale_out(1, 0)
                 scale_out(1, 1)
                 quantize_w("k")
                 mm(0, 2)
                 quantize_w("q10")
+                quantize_x(1, 1)
+                quantize_x(1, 0)
                 quantize_w("q11")
                 mm(0, 3)
                 mm(0, 4)
-                quantize_x(1, 1)
-                quantize_x(1, 0)
+                rot_k(0, 2)
                 quantize_w("v")
+                add_k(0, 2)
                 mm(0, 5)
                 transposes(2, 1)
                 planes(2, 1)
-                rot_k(0, 2)
-                add_k(0, 2)
             else:
-                if more:
+                if not wide:
                     scale_out(n + 1, 0)
+                if n + 2 in WOVEN0:
+                    transposes(n + 2, 0)
+                    planes(n + 2, 0)
                 rot_k(n, 2)
-                if more:
-                    quantize_x(n + 1, 1)
-                    quantize_x(n + 1, 0)
+                if wide:
+                    add_store(n, 1, late_add[0], late_add[1], True)
+                quantize_x(n + 1, 1)
+                quantize_x(n + 1, 0)
                 add_k(n, 2)
-            if more:
-                mm(n + 1, 0)
-                mm(n + 1, 1)
-                mm(n + 1, 2)
+            mm(n + 1, 0)
+            mm(n + 1, 1)
+            mm(n + 1, 2)
             if n + 2 < NPAIR:
-                transposes(n + 2, 0)
+                if n + 2 not in WOVEN0:
+                    transposes(n + 2, 0)
                 weave(n + 2, 1)
             finish(n, 5)
             if n + 2 < NPAIR:
                 weave_out(n + 2, 1)
+            if n + 2 in WOVEN0:
+                weave(n + 2, 0)
+                weave_out(n + 2, 0)
             if n + 4 < NPAIR:
                 cast(n + 4)
             finish(n, 3)
-            if more:
-                mm(n + 1, 3)
-            finish(n, 4, not more)
-            if more:
-                mm(n + 1, 4)
-                mm(n + 1, 5)
+            mm(n + 1, 3)
+            finish(n, 4)
+            mm(n + 1, 4)
+            mm(n + 1, 5)
+
+        last = NPAIR - 1
+        finish(last, 5)
+        finish(last, 0)
+        finish(last, 1)
+        finish(last, 3)
+        ta, tb = finish(last, 4, True)
+        rot_k(last, 2)
+        add_store(last, 4, ta, tb, True)
+        add_k(last, 2, True)

@@ -19,8 +19,7 @@ P = 128
 NT = T // P
 NPAIR = NT // 2
 UNITS = (("q", 0, 0), ("q", 1, 0), ("k", 0, 0), ("q", 0, 1), ("q", 1, 1), ("v", 0, 0))
-XS = (2, 3, 4, 5, 6, 7)
-WOVEN0 = (7,)
+WOVEN0 = (3, 5, 7)
 COPY = mybir.ActivationFunctionType.Copy
 
 
@@ -276,7 +275,7 @@ def tile_attention_pa_kernel(
                         in_=o[:, h * 256 : (h + 1) * 256].rearrange("p (a f) -> p a f", a=2),
                     )
 
-        def rot_k(n, u):
+        def rot_k_cos(n, u):
             a = acc[(n, u)]
             ta = rope.tile([P, 512], F32, name="ta", tag="ta")
             tb = rope.tile([P, 512], F32, name="tb", tag="tb")
@@ -289,8 +288,13 @@ def tile_attention_pa_kernel(
                 in1=cosr[:, 2 * n : 2 * n + 2, :].rearrange("p i j -> p (i j)").unsqueeze(1).unsqueeze(3).to_broadcast(shape),
                 op=MULT,
             )
+
+        def rot_k_sin(n, u):
+            a = acc[(n, u)]
+            pat = "p (h j e) -> p h j e"
+            shape = [P, 2, 128, 2]
             nc.vector.tensor_tensor(
-                out=tb[:].rearrange(pat, j=128, e=2),
+                out=kt[n][1][:].rearrange(pat, j=128, e=2),
                 in0=a[:].rearrange(pat, j=128, e=2)[:, :, :, ::-1],
                 in1=ss[:, :, 2 * n : 2 * n + 2, :].rearrange("p e i j -> p (i j) e").unsqueeze(1).to_broadcast(shape),
                 op=MULT,
@@ -317,14 +321,14 @@ def tile_attention_pa_kernel(
         cast(0, True)
         transposes(0, 0)
         transposes(0, 1)
-        interleave_w("q00", "s")
+        interleave_w("q00", "v")
         interleave_w("q01", "v")
         scale_out(0, 0)
         scale_out(0, 1)
-        quantize_x(0, 0)
         quantize_w("q00")
-        quantize_x(0, 1)
         quantize_w("q01")
+        quantize_x(0, 0)
+        quantize_x(0, 1)
         cast(1)
         nc.vector.tensor_scalar(out=ss[:, 0, :, :], in0=ss[:, 1, :, :], scalar1=-1.0, scalar2=0.0, op0=MULT, op1=ADD)
         interleave_w("k", "s")
@@ -338,52 +342,68 @@ def tile_attention_pa_kernel(
         transposes(1, 0)
         transposes(1, 1)
 
-        for n in range(NPAIR - 1):
-            early = (n + 2 in XS) and (n + 1 in XS)
-            if early:
+        quantize_w("k")
+        finish(0, 0)
+        finish(0, 1)
+        scale_out(1, 0)
+        scale_out(1, 1)
+        mm(0, 2)
+        quantize_w("q10")
+        quantize_w("q11")
+        rot_k_cos(0, 2)
+        mm(0, 3)
+        mm(0, 4)
+        quantize_x(1, 1)
+        quantize_x(1, 0)
+        rot_k_sin(0, 2)
+        add_k(0, 2)
+        mm(1, 0)
+        mm(1, 1)
+        quantize_w("v")
+        mm(0, 5)
+        transposes(2, 1)
+        planes(2, 1)
+        mm(1, 2)
+        transposes(2, 0)
+        weave(2, 1)
+        finish(0, 5)
+        weave_out(2, 1)
+        cast(4)
+        finish(0, 3)
+        mm(1, 3)
+        finish(0, 4)
+        mm(1, 4)
+        mm(1, 5)
+
+        for n in range(1, NPAIR - 1):
+            ahead = n + 2 < NPAIR
+            wide = n + 1 in WOVEN0
+            if ahead:
                 transposes(n + 2, 1)
                 planes(n + 2, 1)
             finish(n, 0)
-            wide = n + 1 in WOVEN0
             late_add = finish(n, 1, wide)
-            if n == 0:
-                scale_out(1, 0)
-                scale_out(1, 1)
-                quantize_w("k")
-                mm(0, 2)
-                quantize_w("q10")
-                quantize_x(1, 1)
-                quantize_x(1, 0)
-                quantize_w("q11")
-                mm(0, 3)
-                mm(0, 4)
-                rot_k(0, 2)
-                quantize_w("v")
-                add_k(0, 2)
-                mm(0, 5)
-                transposes(2, 1)
-                planes(2, 1)
-            else:
-                if not wide:
-                    scale_out(n + 1, 0)
-                if n + 2 in WOVEN0:
-                    transposes(n + 2, 0)
-                    planes(n + 2, 0)
-                rot_k(n, 2)
-                if wide:
-                    add_store(n, 1, late_add[0], late_add[1], True)
-                quantize_x(n + 1, 1)
-                quantize_x(n + 1, 0)
-                add_k(n, 2)
+            if not wide:
+                scale_out(n + 1, 0)
+            if n + 2 in WOVEN0:
+                transposes(n + 2, 0)
+                planes(n + 2, 0)
+            rot_k_cos(n, 2)
+            if wide:
+                add_store(n, 1, late_add[0], late_add[1], True)
+            rot_k_sin(n, 2)
+            quantize_x(n + 1, 1)
+            quantize_x(n + 1, 0)
+            add_k(n, 2)
             mm(n + 1, 0)
             mm(n + 1, 1)
             mm(n + 1, 2)
-            if n + 2 < NPAIR:
+            if ahead:
                 if n + 2 not in WOVEN0:
                     transposes(n + 2, 0)
                 weave(n + 2, 1)
             finish(n, 5)
-            if n + 2 < NPAIR:
+            if ahead:
                 weave_out(n + 2, 1)
             if n + 2 in WOVEN0:
                 weave(n + 2, 0)
@@ -402,6 +422,7 @@ def tile_attention_pa_kernel(
         finish(last, 1)
         finish(last, 3)
         ta, tb = finish(last, 4, True)
-        rot_k(last, 2)
+        rot_k_cos(last, 2)
+        rot_k_sin(last, 2)
         add_store(last, 4, ta, tb, True)
         add_k(last, 2, True)

@@ -34,7 +34,7 @@ def tile_attention_pa_kernel(
         xbp = ctx.enter_context(tc.tile_pool(name="xbp", bufs=1))
         xwork = ctx.enter_context(tc.tile_pool(name="xwork", bufs=3))
         rope = ctx.enter_context(tc.tile_pool(name="rope", bufs=4))
-        outp = ctx.enter_context(tc.tile_pool(name="outp", bufs=5))
+        outp = ctx.enter_context(tc.tile_pool(name="outp", bufs=7))
         accp = ctx.enter_context(tc.psum_pool(name="accp", bufs=6))
         xtp = ctx.enter_context(tc.psum_pool(name="xtp", bufs=1))
 
@@ -69,14 +69,15 @@ def tile_attention_pa_kernel(
                 in_=w.rearrange("(g p t) n -> p g t n", p=P, t=4),
             )
 
-        load_x(0)
+        for tl in range(2):
+            nc.sync.dma_start(out=xb[0][:, tl, :], in_=xb_v[:, tl, :])
         nc.sync.dma_start(out=sc[:], in_=x_scale.rearrange("o (g p t) -> p (o g) t", p=P, t=4))
         load_wq(0, 0)
         load_wq(0, 1)
         load_x(1)
+        load_wkv("k", wk)
         nc.sync.dma_start(out=cosr[:], in_=freqs_cos.rearrange("(p i) j -> p i j", i=NT))
         nc.sync.dma_start(out=ss[:, 1, :, :], in_=freqs_sin.rearrange("(p i) j -> p i j", i=NT))
-        load_wkv("k", wk)
         load_wq(1, 0)
         load_wq(1, 1)
         load_wkv("v", wv)
@@ -103,7 +104,10 @@ def tile_attention_pa_kernel(
             else:
                 o = grouped[:].rearrange("p (c i t) -> p c t i", i=4, t=4)
                 i = wraw[key][:].rearrange("p (t c i) -> p c t i", t=4, i=4)
-            if eng == "v":
+            if eng == "half":
+                nc.vector.tensor_copy(out=o[:, 0:64], in_=i[:, 0:64])
+                nc.scalar.copy(out=o[:, 64:128], in_=i[:, 64:128])
+            elif eng == "v":
                 nc.vector.tensor_copy(out=o, in_=i)
             elif eng == "g":
                 nc.gpsimd.tensor_scalar(out=o, in0=i, scalar1=1.0, scalar2=0.0, op0=MULT, op1=ADD)
@@ -126,20 +130,23 @@ def tile_attention_pa_kernel(
         il = {}
         acc = {}
 
-        def cast(n, on_vector=False):
+        def cast_half(tl):
+            if 0 not in xbf:
+                xbf[0] = xwork.tile([P, 2 * DIM], BF16, name="xbf", tag="xbf")
+            nc.vector.tensor_copy(out=xbf[0][:, tl * DIM : (tl + 1) * DIM], in_=xb[0][:, tl, :].bitcast(FP8))
+
+        def cast(n):
             t = xwork.tile([P, 2 * DIM], BF16, name="xbf", tag="xbf")
             xbf[n] = t
-            if on_vector:
-                nc.vector.tensor_copy(out=t[:], in_=xb[n][:].rearrange("p i k -> p (i k)").bitcast(FP8))
-            else:
-                nc.scalar.copy(out=t[:], in_=xb[n][:].rearrange("p i k -> p (i k)").bitcast(FP8))
+            nc.scalar.copy(out=t[:], in_=xb[n][:].rearrange("p i k -> p (i k)").bitcast(FP8))
 
-        def transposes(n, g):
+        def transposes(n, g, tls=(0, 1)):
             words = xbf[n][:].bitcast(F32)
-            t = xtp.tile([P, 2, 256], F32, name="xt%d" % g, tag="xt%d" % g)
-            xt[(n, g)] = t
+            if (n, g) not in xt:
+                xt[(n, g)] = xtp.tile([P, 2, 256], F32, name="xt%d" % g, tag="xt%d" % g)
+            t = xt[(n, g)]
             for u in range(2):
-                for tl in range(2):
+                for tl in tls:
                     lo = tl * 512 + 256 * g + u
                     nc.tensor.transpose(
                         t[:, u, tl * P : (tl + 1) * P],
@@ -318,12 +325,13 @@ def tile_attention_pa_kernel(
                 add_store(n, u, ta, tb, False)
             return ta, tb
 
-        cast(0, True)
-        transposes(0, 0)
-        transposes(0, 1)
-        interleave_w("q00", "v")
-        interleave_w("q01", "v")
+        for tl in range(2):
+            cast_half(tl)
+            transposes(0, 0, (tl,))
+            transposes(0, 1, (tl,))
+        interleave_w("q00", "half")
         scale_out(0, 0)
+        interleave_w("q01", "v")
         scale_out(0, 1)
         quantize_w("q00")
         quantize_w("q01")
@@ -425,4 +433,12 @@ def tile_attention_pa_kernel(
         rot_k_cos(last, 2)
         rot_k_sin(last, 2)
         add_store(last, 4, ta, tb, True)
-        add_k(last, 2, True)
+        ta, tb = kt[last]
+        o = outp.tile([P, 512], F32, name="o", tag="o")
+        for h in range(2):
+            part = slice(h * 256, (h + 1) * 256)
+            nc.vector.tensor_tensor(out=o[:, part], in0=ta[:, part], in1=tb[:, part], op=ADD)
+            nc.sync.dma_start(
+                out=k_v[:, 2 * last : 2 * last + 2, h * P : (h + 1) * P],
+                in_=o[:, part].rearrange("p (a f) -> p a f", a=2),
+            )

@@ -71,8 +71,8 @@ def tile_attention_pa_kernel(
 
         for tl in range(2):
             nc.sync.dma_start(out=xb[0][:, tl, :], in_=xb_v[:, tl, :])
-        nc.sync.dma_start(out=sc[:], in_=x_scale.rearrange("o (g p t) -> p (o g) t", p=P, t=4))
         load_wq(0, 0)
+        nc.sync.dma_start(out=sc[:], in_=x_scale.rearrange("o (g p t) -> p (o g) t", p=P, t=4))
         load_wq(0, 1)
         load_x(1)
         load_wkv("k", wk)
@@ -340,7 +340,7 @@ def tile_attention_pa_kernel(
         cast(1)
         nc.vector.tensor_scalar(out=ss[:, 0, :, :], in0=ss[:, 1, :, :], scalar1=-1.0, scalar2=0.0, op0=MULT, op1=ADD)
         interleave_w("k", "s")
-        interleave_w("q10", "s")
+        interleave_w("q10", "half")
         interleave_w("q11", "s")
         interleave_w("v", "s")
         cast(2)

@@ -19,7 +19,7 @@ P = 128
 NT = T // P
 NPAIR = NT // 2
 UNITS = (("q", 0, 0), ("q", 1, 0), ("k", 0, 0), ("q", 0, 1), ("q", 1, 1), ("v", 0, 0))
-WOVEN0 = (3, 5, 7)
+WOVEN0 = (3, 5, 6, 7)
 COPY = mybir.ActivationFunctionType.Copy
 
 

from contextlib import ExitStack

import concourse.mybir as mybir
from concourse.masks import make_identity

F32 = mybir.dt.float32
BF16 = mybir.dt.bfloat16
U32 = mybir.dt.uint32
U8 = mybir.dt.uint8
FP8 = mybir.dt.float8_e4m3fn
FP8X4 = mybir.dt.float8_e4m3fn_x4
MULT = mybir.AluOpType.mult
ADD = mybir.AluOpType.add

T, DIM, HD = 2048, 1024, 128
FLOPS = 2 * T * DIM * 1536

P = 128
NT = T // P
NPAIR = NT // 2
UNITS = (("q", 0, 0), ("q", 1, 0), ("k", 0, 0), ("q", 0, 1), ("q", 1, 1), ("v", 0, 0))
WOVEN0 = (3, 5, 6, 7)
COPY = mybir.ActivationFunctionType.Copy


def tile_attention_pa_kernel(
    tc, x_bytes, x_scale, freqs_cos, freqs_sin, wq, wk, wv, out_0, out_1, out_2
):
    nc = tc.nc
    with ExitStack() as ctx:
        ctx.enter_context(tc.manual_schedule())
        const = ctx.enter_context(tc.tile_pool(name="const", bufs=1))
        wpool = ctx.enter_context(tc.tile_pool(name="wpool", bufs=1))
        xbp = ctx.enter_context(tc.tile_pool(name="xbp", bufs=1))
        xwork = ctx.enter_context(tc.tile_pool(name="xwork", bufs=3))
        rope = ctx.enter_context(tc.tile_pool(name="rope", bufs=4))
        outp = ctx.enter_context(tc.tile_pool(name="outp", bufs=7))
        accp = ctx.enter_context(tc.psum_pool(name="accp", bufs=6))
        xtp = ctx.enter_context(tc.psum_pool(name="xtp", bufs=1))

        xb_v = x_bytes.rearrange("(p i) k -> p i k", i=NT)
        q_v = out_0.rearrange("(p i) h d -> p i (h d)", i=NT)
        k_v = out_1.rearrange("(p i) h d -> p i (h d)", i=NT)
        v_v = out_2.rearrange("(p i) h d -> p i (h d)", i=NT)
        wq_v = wq.rearrange("(g p t) n -> g p t n", p=P, t=4)

        xb = []
        for n in range(NPAIR):
            xb.append(xbp.tile([P, 2, DIM], U8, name="xbytes%d" % n, tag="xbytes%d" % n))
        sc = const.tile([P, 2, 4], F32, name="sc", tag="sc")
        cosr = const.tile([P, NT, 64], BF16, name="cosr", tag="cosr")
        ss = const.tile([P, 2, NT, 64], BF16, name="ss", tag="ss")
        wraw = {}
        for key in ("q00", "q01", "q10", "q11", "k", "v"):
            wraw[key] = wpool.tile([P, 2048], BF16, name="wraw" + key, tag="wraw" + key)

        def load_x(n):
            nc.sync.dma_start(out=xb[n][:], in_=xb_v[:, 2 * n : 2 * n + 2, :])

        def load_wq(c, g):
            nc.sync.dma_start(
                out=wraw["q%d%d" % (c, g)][:].rearrange("p (t n) -> p t n", t=4),
                in_=wq_v[g][:, :, c * 512 : (c + 1) * 512],
            )

        def load_wkv(key, w):
            nc.sync.dma_start(
                out=wraw[key][:].rearrange("p (g t n) -> p g t n", g=2, t=4),
                in_=w.rearrange("(g p t) n -> p g t n", p=P, t=4),
            )

        for tl in range(2):
            nc.sync.dma_start(out=xb[0][:, tl, :], in_=xb_v[:, tl, :])
        load_wq(0, 0)
        nc.sync.dma_start(out=sc[:], in_=x_scale.rearrange("o (g p t) -> p (o g) t", p=P, t=4))
        load_wq(0, 1)
        load_x(1)
        load_wkv("k", wk)
        nc.sync.dma_start(out=cosr[:], in_=freqs_cos.rearrange("(p i) j -> p i j", i=NT))
        nc.sync.dma_start(out=ss[:, 1, :, :], in_=freqs_sin.rearrange("(p i) j -> p i j", i=NT))
        load_wq(1, 0)
        load_wq(1, 1)
        load_wkv("v", wv)
        for n in range(2, NPAIR):
            load_x(n)

        ident = const.tile([P, P], F32, name="ident", tag="ident")
        make_identity(nc, ident[:])
        identb = const.tile([P, P], BF16, name="identb", tag="identb")
        make_identity(nc, identb[:])
        warm = const.tile([P, 1], F32, name="warm", tag="warm")
        nc.scalar.activation(out=warm[:], in_=ident[:, 0:1], func=COPY)

        wc = {}
        ws = {}
        wg = {}

        def interleave_w(key, eng):
            grouped = wpool.tile([P, 2048], BF16, name="wg" + key, tag="wg" + key, align_bytes=64)
            wg[key] = grouped
            if key in ("k", "v"):
                o = grouped[:].rearrange("p (g n t) -> p g n t", g=2, t=4)
                i = wraw[key][:].rearrange("p (g t n) -> p g n t", g=2, t=4)
            else:
                o = grouped[:].rearrange("p (c i t) -> p c t i", i=4, t=4)
                i = wraw[key][:].rearrange("p (t c i) -> p c t i", t=4, i=4)
            if eng == "half":
                nc.vector.tensor_copy(out=o[:, 0:64], in_=i[:, 0:64])
                nc.scalar.copy(out=o[:, 64:128], in_=i[:, 64:128])
            elif eng == "v":
                nc.vector.tensor_copy(out=o, in_=i)
            elif eng == "g":
                nc.gpsimd.tensor_scalar(out=o, in0=i, scalar1=1.0, scalar2=0.0, op0=MULT, op1=ADD)
            else:
                nc.scalar.copy(out=o, in_=i)

        def quantize_w(key):
            codes = wpool.tile([P, 512], U32, name="wc" + key, tag="wc" + key, align_bytes=64)
            scales = wpool.tile([P, 512], U8, name="ws" + key, tag="ws" + key, align_bytes=64)
            wc[key] = codes
            ws[key] = scales
            nc.vector.quantize_mx(out=codes[:].bitcast(FP8X4), scales=scales[:], in_=wg[key][:])

        xbf = {}
        xt = {}
        xg = {}
        xc = {}
        xs = {}
        pl = {}
        il = {}
        acc = {}

        def cast_half(tl):
            if 0 not in xbf:
                xbf[0] = xwork.tile([P, 2 * DIM], BF16, name="xbf", tag="xbf")
            nc.vector.tensor_copy(out=xbf[0][:, tl * DIM : (tl + 1) * DIM], in_=xb[0][:, tl, :].bitcast(FP8))

        def cast(n):
            t = xwork.tile([P, 2 * DIM], BF16, name="xbf", tag="xbf")
            xbf[n] = t
            nc.scalar.copy(out=t[:], in_=xb[n][:].rearrange("p i k -> p (i k)").bitcast(FP8))

        def transposes(n, g, tls=(0, 1)):
            words = xbf[n][:].bitcast(F32)
            if (n, g) not in xt:
                xt[(n, g)] = xtp.tile([P, 2, 256], F32, name="xt%d" % g, tag="xt%d" % g)
            t = xt[(n, g)]
            for u in range(2):
                for tl in tls:
                    lo = tl * 512 + 256 * g + u
                    nc.tensor.transpose(
                        t[:, u, tl * P : (tl + 1) * P],
                        words[:, lo : tl * 512 + 256 * (g + 1) : 2],
                        ident[:],
                    )

        def planes(n, g):
            t4 = xwork.tile([P, 4, 256], BF16, name="pl%d" % g, tag="pl%d" % g)
            pl[(n, g)] = t4
            src = xt[(n, g)][:].rearrange("p u r -> p (u r)").bitcast(BF16).rearrange("p (u r e) -> p u r e", u=2, e=2)
            for t in range(4):
                nc.scalar.activation(
                    out=t4[:, t, :], in_=src[:, t // 2, :, t % 2], func=COPY, scale=sc[:, g, t : t + 1]
                )

        def weave(n, g):
            bank = xtp.tile([P, 1024], BF16, name="xt%d" % g, tag="xt%d" % g)
            il[(n, g)] = bank
            for h in range(2):
                nc.tensor.matmul(
                    bank[:, h * 512 : (h + 1) * 512],
                    lhsT=identb[:],
                    rhs=pl[(n, g)][:, :, h * P : (h + 1) * P].rearrange("p t r -> p r t"),
                    start=True,
                    stop=True,
                )

        def weave_out(n, g):
            if n not in xg:
                xg[n] = xwork.tile([P, 2048], BF16, name="xg", tag="xg", align_bytes=64)
            nc.scalar.copy(out=xg[n][:, g * 1024 : (g + 1) * 1024], in_=il[(n, g)][:])

        def scale_out(n, g):
            if n not in xg:
                xg[n] = xwork.tile([P, 2048], BF16, name="xg", tag="xg", align_bytes=64)
            src = xt[(n, g)][:].rearrange("p u r -> p (u r)").bitcast(BF16)
            nc.vector.tensor_tensor(
                out=xg[n][:, g * 1024 : (g + 1) * 1024].rearrange("p (r u e) -> p r u e", u=2, e=2),
                in0=src.rearrange("p (u r e) -> p r u e", u=2, e=2),
                in1=sc[:, g, :].rearrange("p (u e) -> p u e", e=2).unsqueeze(1).to_broadcast([P, 256, 2, 2]),
                op=MULT,
            )

        def quantize_x(n, g):
            if n not in xc:
                xc[n] = xwork.tile([P, 512], U32, name="xc", tag="xc", align_bytes=64)
                xs[n] = xwork.tile([P, 512], U8, name="xs", tag="xs", align_bytes=64)
            nc.vector.quantize_mx(
                out=xc[n][:, g * 256 : (g + 1) * 256].bitcast(FP8X4),
                scales=xs[n][:, g * 256 : (g + 1) * 256],
                in_=xg[n][:, g * 1024 : (g + 1) * 1024],
            )

        def mm(n, u):
            kind, tl, c = UNITS[u]
            a = accp.tile([P, 512], F32, name="acc", tag="acc")
            acc[(n, u)] = a
            if kind == "q":
                for g in range(2):
                    cols = slice(g * 256 + tl * P, g * 256 + (tl + 1) * P)
                    key = "q%d%d" % (c, g)
                    nc.tensor.matmul_mx(
                        out=a[:],
                        lhsT=xc[n][:, cols].bitcast(FP8X4),
                        lhsT_scale=xs[n][:, cols],
                        rhs=wc[key][:].bitcast(FP8X4),
                        rhs_scale=ws[key][:],
                        start=(g == 0),
                        stop=(g == 1),
                    )
            elif kind == "v":
                for t2 in range(2):
                    for g in range(2):
                        cols = slice(g * 256 + t2 * P, g * 256 + (t2 + 1) * P)
                        wcols = slice(g * 256, (g + 1) * 256)
                        nc.tensor.matmul_mx(
                            out=a[:, t2 * 256 : (t2 + 1) * 256],
                            lhsT=xc[n][:, cols].bitcast(FP8X4),
                            lhsT_scale=xs[n][:, cols],
                            rhs=wc[kind][:, wcols].bitcast(FP8X4),
                            rhs_scale=ws[kind][:, wcols],
                            start=(g == 0),
                            stop=(g == 1),
                        )
            else:
                for t2 in range(2):
                    for h in range(2):
                        for g in range(2):
                            cols = slice(g * 256 + t2 * P, g * 256 + (t2 + 1) * P)
                            wcols = slice(g * 256 + h * P, g * 256 + (h + 1) * P)
                            nc.tensor.matmul_mx(
                                out=a[:, h * 256 + t2 * P : h * 256 + (t2 + 1) * P],
                                lhsT=xc[n][:, cols].bitcast(FP8X4),
                                lhsT_scale=xs[n][:, cols],
                                rhs=wc[kind][:, wcols].bitcast(FP8X4),
                                rhs_scale=ws[kind][:, wcols],
                                start=(g == 0),
                                stop=(g == 1),
                            )

        def rot_part(a_ap, b_ap, u_ap, i, nh):
            pat = "p (h j e) -> p h j e"
            shape = [P, nh, 64, 2]
            nc.vector.tensor_tensor(
                out=a_ap.rearrange(pat, j=64, e=2),
                in0=u_ap.rearrange(pat, j=64, e=2),
                in1=cosr[:, i, :].unsqueeze(1).unsqueeze(3).to_broadcast(shape),
                op=MULT,
            )
            nc.vector.tensor_tensor(
                out=b_ap.rearrange(pat, j=64, e=2),
                in0=u_ap.rearrange(pat, j=64, e=2)[:, :, :, ::-1],
                in1=ss[:, :, i, :].rearrange("p e j -> p j e").unsqueeze(1).to_broadcast(shape),
                op=MULT,
            )

        kt = {}

        def add_store(n, u, ta, tb, on_vector):
            kind, tl, c = UNITS[u]
            o = outp.tile([P, 512], F32, name="o", tag="o")
            if on_vector:
                nc.vector.tensor_tensor(out=o[:], in0=ta[:], in1=tb[:], op=ADD)
            else:
                nc.gpsimd.tensor_tensor(out=o[:], in0=ta[:], in1=tb[:], op=ADD)
            if kind == "q":
                nc.sync.dma_start(out=q_v[:, 2 * n + tl, c * 512 : (c + 1) * 512], in_=o[:])
            else:
                for h in range(2):
                    nc.sync.dma_start(
                        out=k_v[:, 2 * n : 2 * n + 2, h * P : (h + 1) * P],
                        in_=o[:, h * 256 : (h + 1) * 256].rearrange("p (a f) -> p a f", a=2),
                    )

        def rot_k_cos(n, u):
            a = acc[(n, u)]
            ta = rope.tile([P, 512], F32, name="ta", tag="ta")
            tb = rope.tile([P, 512], F32, name="tb", tag="tb")
            kt[n] = (ta, tb)
            pat = "p (h j e) -> p h j e"
            shape = [P, 2, 128, 2]
            nc.vector.tensor_tensor(
                out=ta[:].rearrange(pat, j=128, e=2),
                in0=a[:].rearrange(pat, j=128, e=2),
                in1=cosr[:, 2 * n : 2 * n + 2, :].rearrange("p i j -> p (i j)").unsqueeze(1).unsqueeze(3).to_broadcast(shape),
                op=MULT,
            )

        def rot_k_sin(n, u):
            a = acc[(n, u)]
            pat = "p (h j e) -> p h j e"
            shape = [P, 2, 128, 2]
            nc.vector.tensor_tensor(
                out=kt[n][1][:].rearrange(pat, j=128, e=2),
                in0=a[:].rearrange(pat, j=128, e=2)[:, :, :, ::-1],
                in1=ss[:, :, 2 * n : 2 * n + 2, :].rearrange("p e i j -> p (i j) e").unsqueeze(1).to_broadcast(shape),
                op=MULT,
            )

        def add_k(n, u, on_vector=False):
            add_store(n, u, kt[n][0], kt[n][1], on_vector)

        def finish(n, u, later=False):
            kind, tl, c = UNITS[u]
            a = acc[(n, u)]
            if kind == "v":
                o = outp.tile([P, 512], F32, name="ov", tag="ov")
                nc.scalar.copy(out=o[:], in_=a[:])
                nc.scalar.dma_start(out=v_v[:, 2 * n : 2 * n + 2, :], in_=o[:].rearrange("p (a f) -> p a f", a=2))
                return
            ta = rope.tile([P, 512], F32, name="ta", tag="ta")
            tb = rope.tile([P, 512], F32, name="tb", tag="tb")
            rot_part(ta[:], tb[:], a[:], 2 * n + tl, 4)
            if not later:
                add_store(n, u, ta, tb, False)
            return ta, tb

        for tl in range(2):
            cast_half(tl)
            transposes(0, 0, (tl,))
            transposes(0, 1, (tl,))
        interleave_w("q00", "half")
        scale_out(0, 0)
        interleave_w("q01", "v")
        scale_out(0, 1)
        quantize_w("q00")
        quantize_w("q01")
        quantize_x(0, 0)
        quantize_x(0, 1)
        cast(1)
        nc.vector.tensor_scalar(out=ss[:, 0, :, :], in0=ss[:, 1, :, :], scalar1=-1.0, scalar2=0.0, op0=MULT, op1=ADD)
        interleave_w("k", "s")
        interleave_w("q10", "half")
        interleave_w("q11", "s")
        interleave_w("v", "s")
        cast(2)
        cast(3)
        mm(0, 0)
        mm(0, 1)
        transposes(1, 0)
        transposes(1, 1)

        quantize_w("k")
        finish(0, 0)
        finish(0, 1)
        scale_out(1, 0)
        scale_out(1, 1)
        mm(0, 2)
        quantize_w("q10")
        quantize_w("q11")
        rot_k_cos(0, 2)
        mm(0, 3)
        mm(0, 4)
        quantize_x(1, 1)
        quantize_x(1, 0)
        rot_k_sin(0, 2)
        add_k(0, 2)
        mm(1, 0)
        mm(1, 1)
        quantize_w("v")
        mm(0, 5)
        transposes(2, 1)
        planes(2, 1)
        mm(1, 2)
        transposes(2, 0)
        weave(2, 1)
        finish(0, 5)
        weave_out(2, 1)
        cast(4)
        finish(0, 3)
        mm(1, 3)
        finish(0, 4)
        mm(1, 4)
        mm(1, 5)

        for n in range(1, NPAIR - 1):
            ahead = n + 2 < NPAIR
            wide = n + 1 in WOVEN0
            if ahead:
                transposes(n + 2, 1)
                planes(n + 2, 1)
            finish(n, 0)
            late_add = finish(n, 1, wide)
            if not wide:
                scale_out(n + 1, 0)
            if n + 2 in WOVEN0:
                transposes(n + 2, 0)
                planes(n + 2, 0)
            rot_k_cos(n, 2)
            if wide:
                add_store(n, 1, late_add[0], late_add[1], True)
            rot_k_sin(n, 2)
            quantize_x(n + 1, 1)
            quantize_x(n + 1, 0)
            add_k(n, 2)
            mm(n + 1, 0)
            mm(n + 1, 1)
            mm(n + 1, 2)
            if ahead:
                if n + 2 not in WOVEN0:
                    transposes(n + 2, 0)
                weave(n + 2, 1)
            finish(n, 5)
            if ahead:
                weave_out(n + 2, 1)
            if n + 2 in WOVEN0:
                weave(n + 2, 0)
                weave_out(n + 2, 0)
            if n + 4 < NPAIR:
                cast(n + 4)
            finish(n, 3)
            mm(n + 1, 3)
            finish(n, 4)
            mm(n + 1, 4)
            mm(n + 1, 5)

        last = NPAIR - 1
        finish(last, 5)
        finish(last, 0)
        finish(last, 1)
        finish(last, 3)
        ta, tb = finish(last, 4, True)
        rot_k_cos(last, 2)
        rot_k_sin(last, 2)
        add_store(last, 4, ta, tb, True)
        ta, tb = kt[last]
        o = outp.tile([P, 512], F32, name="o", tag="o")
        for h in range(2):
            part = slice(h * 256, (h + 1) * 256)
            nc.vector.tensor_tensor(out=o[:, part], in0=ta[:, part], in1=tb[:, part], op=ADD)
            nc.sync.dma_start(
                out=k_v[:, 2 * last : 2 * last + 2, h * P : (h + 1) * P],
                in_=o[:, part].rearrange("p (a f) -> p a f", a=2),
            )
